import numpy as np
import ml_dtypes

BF16 = ml_dtypes.bfloat16


def bf(x):
    return np.asarray(x, np.float32).astype(BF16)


def f32(x):
    return np.asarray(x, np.float32)


def f64(x):
    return np.asarray(x).astype(np.float64)


def striped(idx):
    return np.tile(idx.reshape(-1, 16).T, (8, 1))


D, S, N, E = 128, 256, 128, 128
SCALE = 1.0 / np.sqrt(D)


def setup_inputs():
    return {"q": bf(np.random.standard_normal((D, E))), "pool_k": bf(np.random.standard_normal((D, S))), "k": bf(np.random.standard_normal((D, E))), "vals": bf(2.0 * np.random.standard_normal((N + E, D))), "offs": striped(np.random.permutation(S)[:N])}


def reference(q, pool_k, k, vals, offs):
    idx = offs[:16].T.reshape(-1)
    sp = SCALE * (f64(q).T @ f64(pool_k)[:, idx])
    sn = SCALE * (f64(q).T @ f64(k))
    seen = np.arange(E)[None, :] <= np.arange(E)[:, None]
    e = np.concatenate([np.exp(sp), np.where(seen, np.exp(sn), 0.0)], axis=1)
    return (e @ f64(vals)) / e.sum(axis=1, keepdims=True)

@@ -1,0 +1,67 @@
+import math
+
+import concourse.mybir as mybir
+from concourse.masks import make_identity
+
+D, S, N, E = 128, 256, 128, 128
+SCALE = 1.0 / math.sqrt(D)
+MASKED = -1.0e30
+FLOPS = 2 * E * (N + E) * D + 2 * E * (N + E) * D
+
+BF16, F32, I32, U16 = mybir.dt.bfloat16, mybir.dt.float32, mybir.dt.int32, mybir.dt.uint16
+ALU = mybir.AluOpType
+EXP = mybir.ActivationFunctionType.Exp
+X = mybir.AxisListType.X
+
+
+def tile_radixattention_kernel(tc, q, pool_k, k, vals, offs, out):
+    nc = tc.nc
+    with (
+        tc.tile_pool(name="held", bufs=1) as held,
+        tc.psum_pool(name="psum", bufs=1) as psum,
+    ):
+        offsets = held.tile([128, N // 16], U16, name="offsets")
+        nc.sync.dma_start(offsets[:], offs)
+        pool_sb = held.tile([D, S], BF16, name="pool_sb")
+        nc.sync.dma_start(pool_sb[:], pool_k)
+        q_sb = held.tile([D, E], BF16, name="q_sb")
+        nc.scalar.dma_start(q_sb[:], q)
+        k_sb = held.tile([D, E], BF16, name="k_sb")
+        nc.scalar.dma_start(k_sb[:], k)
+        vals_sb = held.tile([128, 2, D], BF16, name="vals_sb")
+        nc.sync.dma_start(vals_sb[:], vals.rearrange("(h j) d -> j h d", h=2))
+
+        ident = held.tile([128, 128], BF16, name="ident")
+        make_identity(nc, ident[:])
+        ahead = held.tile([E, E], I32, name="ahead")
+        nc.gpsimd.iota(ahead[:], pattern=[[-1, E]], base=0, channel_multiplier=1)
+        causal = held.tile([E, E], BF16, name="causal")
+        nc.vector.tensor_scalar(causal[:], ahead[:], 0.0, MASKED, op0=ALU.is_lt, op1=ALU.mult)
+
+        scores = psum.tile([E, N + E], F32, name="scores")
+        nc.tensor.matmul(scores[:, N:], ident[:], causal[:], start=True, stop=False)
+        nc.tensor.matmul(scores[:, N:], q_sb[:], k_sb[:], start=False, stop=True)
+        nc.tensor.matmul(scores[:, :N], q_sb[:], pool_sb[:].indirect(offsets[:]), start=True, stop=True)
+
+        neg_max = held.tile([E, 1], F32, name="neg_max")
+        nc.vector.reduce_max(neg_max[:], scores[:], axis=X, negate=True)
+        shift = held.tile([E, 1], F32, name="shift")
+        nc.vector.tensor_scalar_mul(shift[:], neg_max[:], SCALE)
+        weights = held.tile([E, N + E], BF16, name="weights")
+        denom = held.tile([E, 1], F32, name="denom")
+        nc.scalar.activation(weights[:], scores[:], EXP, bias=shift[:], scale=SCALE, accum_out=denom[:])
+        recip = held.tile([E, 1], F32, name="recip")
+        nc.vector.reciprocal(recip[:], denom[:])
+
+        weights_t_ps = psum.tile([128, 2, E], BF16, name="weights_t_ps")
+        for h in range(2):
+            nc.tensor.transpose(weights_t_ps[:, h, :], weights[:, h * 128 : (h + 1) * 128], ident[:])
+        weights_t = held.tile([128, 2, E], BF16, name="weights_t")
+        nc.vector.tensor_copy(weights_t[:], weights_t_ps[:])
+        mixed = psum.tile([E, D], F32, name="mixed")
+        for h in range(2):
+            nc.tensor.matmul(mixed[:], weights_t[:, h, :], vals_sb[:, h, :], start=(h == 0), stop=(h == 1))
+
+        out_sb = held.tile([E, D], F32, name="out_sb")
+        nc.vector.tensor_scalar_mul(out_sb[:], mixed[:], recip[:])
+        nc.sync.dma_start(out, out_sb[:])

@@ -13,7 +13,6 @@ ALU = mybir.AluOpType
 EXP = mybir.ActivationFunctionType.Exp
 X = mybir.AxisListType.X
 
-
 def tile_radixattention_kernel(tc, q, pool_k, k, vals, offs, out):
     nc = tc.nc
     with (
@@ -38,30 +37,34 @@ def tile_radixattention_kernel(tc, q, pool_k, k, vals, offs, out):
         causal = held.tile([E, E], BF16, name="causal")
         nc.vector.tensor_scalar(causal[:], ahead[:], 0.0, MASKED, op0=ALU.is_lt, op1=ALU.mult)
 
-        scores = psum.tile([E, N + E], F32, name="scores")
-        nc.tensor.matmul(scores[:, N:], ident[:], causal[:], start=True, stop=False)
-        nc.tensor.matmul(scores[:, N:], q_sb[:], k_sb[:], start=False, stop=True)
-        nc.tensor.matmul(scores[:, :N], q_sb[:], pool_sb[:].indirect(offsets[:]), start=True, stop=True)
+        scores = [psum.tile([E, 128], F32, name=f"scores{h}") for h in range(2)]
+        nc.tensor.matmul(scores[1][:], ident[:], causal[:], start=True, stop=False)
+        nc.tensor.matmul(scores[1][:], q_sb[:], k_sb[:], start=False, stop=True)
+        nc.tensor.matmul(scores[0][:], q_sb[:], pool_sb[:].indirect(offsets[:]), start=True, stop=True)
 
-        neg_max = held.tile([E, 1], F32, name="neg_max")
-        nc.vector.reduce_max(neg_max[:], scores[:], axis=X, negate=True)
+        neg_max = [held.tile([E, 1], F32, name=f"neg_max{h}") for h in range(2)]
+        for h in (1, 0):
+            nc.vector.reduce_max(neg_max[h][:], scores[h][:], axis=X, negate=True)
         shift = held.tile([E, 1], F32, name="shift")
-        nc.vector.tensor_scalar_mul(shift[:], neg_max[:], SCALE)
-        weights = held.tile([E, N + E], BF16, name="weights")
-        denom = held.tile([E, 1], F32, name="denom")
-        nc.scalar.activation(weights[:], scores[:], EXP, bias=shift[:], scale=SCALE, accum_out=denom[:])
-        recip = held.tile([E, 1], F32, name="recip")
-        nc.vector.reciprocal(recip[:], denom[:])
+        nc.vector.tensor_scalar(shift[:], neg_max[0][:], neg_max[1][:], SCALE, op0=ALU.min, op1=ALU.mult)
 
-        weights_t_ps = psum.tile([128, 2, E], BF16, name="weights_t_ps")
-        for h in range(2):
-            nc.tensor.transpose(weights_t_ps[:, h, :], weights[:, h * 128 : (h + 1) * 128], ident[:])
-        weights_t = held.tile([128, 2, E], BF16, name="weights_t")
-        nc.vector.tensor_copy(weights_t[:], weights_t_ps[:])
+        weights = [held.tile([E, 128], BF16, name=f"weights{h}") for h in range(2)]
+        denom = [held.tile([E, 1], F32, name=f"denom{h}") for h in range(2)]
+        weights_t_ps = [psum.tile([128, E], BF16, name=f"weights_t_ps{h}") for h in range(2)]
+        weights_t = [held.tile([128, E], BF16, name=f"weights_t{h}") for h in range(2)]
         mixed = psum.tile([E, D], F32, name="mixed")
         for h in range(2):
-            nc.tensor.matmul(mixed[:], weights_t[:, h, :], vals_sb[:, h, :], start=(h == 0), stop=(h == 1))
+            nc.scalar.activation(weights[h][:], scores[h][:], EXP, bias=shift[:], scale=SCALE, accum_out=denom[h][:])
+        for h in range(2):
+            nc.tensor.transpose(weights_t_ps[h][:], weights[h][:], ident[:])
+        nc.vector.tensor_copy(weights_t[0][:], weights_t_ps[0][:])
+        nc.scalar.copy(weights_t[1][:], weights_t_ps[1][:])
+        for h in range(2):
+            nc.tensor.matmul(mixed[:], weights_t[h][:], vals_sb[:, h, :], start=(h == 0), stop=(h == 1))
 
+        recip = held.tile([E, 1], F32, name="recip")
+        nc.vector.tensor_add(recip[:], denom[0][:], denom[1][:])
+        nc.vector.reciprocal(recip[:], recip[:])
         out_sb = held.tile([E, D], F32, name="out_sb")
         nc.vector.tensor_scalar_mul(out_sb[:], mixed[:], recip[:])
         nc.sync.dma_start(out, out_sb[:])

@@ -19,14 +19,14 @@ def tile_radixattention_kernel(tc, q, pool_k, k, vals, offs, out):
         tc.tile_pool(name="held", bufs=1) as held,
         tc.psum_pool(name="psum", bufs=1) as psum,
     ):
+        q_sb = held.tile([D, E], BF16, name="q_sb")
+        nc.sync.dma_start(q_sb[:], q)
+        k_sb = held.tile([D, E], BF16, name="k_sb")
+        nc.scalar.dma_start(k_sb[:], k)
         offsets = held.tile([128, N // 16], U16, name="offsets")
         nc.sync.dma_start(offsets[:], offs)
         pool_sb = held.tile([D, S], BF16, name="pool_sb")
-        nc.sync.dma_start(pool_sb[:], pool_k)
-        q_sb = held.tile([D, E], BF16, name="q_sb")
-        nc.scalar.dma_start(q_sb[:], q)
-        k_sb = held.tile([D, E], BF16, name="k_sb")
-        nc.scalar.dma_start(k_sb[:], k)
+        nc.scalar.dma_start(pool_sb[:], pool_k)
         vals_sb = held.tile([128, 2, D], BF16, name="vals_sb")
         nc.sync.dma_start(vals_sb[:], vals.rearrange("(h j) d -> j h d", h=2))
 
@@ -37,34 +37,29 @@ def tile_radixattention_kernel(tc, q, pool_k, k, vals, offs, out):
         causal = held.tile([E, E], BF16, name="causal")
         nc.vector.tensor_scalar(causal[:], ahead[:], 0.0, MASKED, op0=ALU.is_lt, op1=ALU.mult)
 
-        scores = [psum.tile([E, 128], F32, name=f"scores{h}") for h in range(2)]
-        nc.tensor.matmul(scores[1][:], ident[:], causal[:], start=True, stop=False)
-        nc.tensor.matmul(scores[1][:], q_sb[:], k_sb[:], start=False, stop=True)
-        nc.tensor.matmul(scores[0][:], q_sb[:], pool_sb[:].indirect(offsets[:]), start=True, stop=True)
+        scores = psum.tile([E, N + E], F32, name="scores")
+        nc.tensor.matmul(scores[:, N:], ident[:], causal[:], start=True, stop=False)
+        nc.tensor.matmul(scores[:, N:], q_sb[:], k_sb[:], start=False, stop=True)
+        nc.tensor.matmul(scores[:, :N], q_sb[:], pool_sb[:].indirect(offsets[:]), start=True, stop=True)
 
-        neg_max = [held.tile([E, 1], F32, name=f"neg_max{h}") for h in range(2)]
-        for h in (1, 0):
-            nc.vector.reduce_max(neg_max[h][:], scores[h][:], axis=X, negate=True)
+        neg_scaled = held.tile([E, N + E], F32, name="neg_scaled")
         shift = held.tile([E, 1], F32, name="shift")
-        nc.vector.tensor_scalar(shift[:], neg_max[0][:], neg_max[1][:], SCALE, op0=ALU.min, op1=ALU.mult)
+        nc.vector.tensor_scalar(neg_scaled[:], scores[:], -SCALE, None, op0=ALU.mult, op1=ALU.min, accum_out=shift[:])
+        weights = held.tile([E, N + E], BF16, name="weights")
+        denom = held.tile([E, 1], F32, name="denom")
+        nc.scalar.activation(weights[:], neg_scaled[:], EXP, bias=shift[:], scale=-1.0, accum_out=denom[:])
+        recip = held.tile([E, 1], F32, name="recip")
+        nc.vector.reciprocal(recip[:], denom[:])
 
-        weights = [held.tile([E, 128], BF16, name=f"weights{h}") for h in range(2)]
-        denom = [held.tile([E, 1], F32, name=f"denom{h}") for h in range(2)]
-        weights_t_ps = [psum.tile([128, E], BF16, name=f"weights_t_ps{h}") for h in range(2)]
-        weights_t = [held.tile([128, E], BF16, name=f"weights_t{h}") for h in range(2)]
+        weights_t_ps = psum.tile([128, 2, E], BF16, name="weights_t_ps")
+        for h in range(2):
+            nc.tensor.transpose(weights_t_ps[:, h, :], weights[:, h * 128 : (h + 1) * 128], ident[:])
+        weights_t = held.tile([128, 2, E], BF16, name="weights_t")
+        nc.vector.tensor_copy(weights_t[:], weights_t_ps[:])
         mixed = psum.tile([E, D], F32, name="mixed")
         for h in range(2):
-            nc.scalar.activation(weights[h][:], scores[h][:], EXP, bias=shift[:], scale=SCALE, accum_out=denom[h][:])
-        for h in range(2):
-            nc.tensor.transpose(weights_t_ps[h][:], weights[h][:], ident[:])
-        nc.vector.tensor_copy(weights_t[0][:], weights_t_ps[0][:])
-        nc.scalar.copy(weights_t[1][:], weights_t_ps[1][:])
-        for h in range(2):
-            nc.tensor.matmul(mixed[:], weights_t[h][:], vals_sb[:, h, :], start=(h == 0), stop=(h == 1))
+            nc.tensor.matmul(mixed[:], weights_t[:, h, :], vals_sb[:, h, :], start=(h == 0), stop=(h == 1))
 
-        recip = held.tile([E, 1], F32, name="recip")
-        nc.vector.tensor_add(recip[:], denom[0][:], denom[1][:])
-        nc.vector.reciprocal(recip[:], recip[:])
         out_sb = held.tile([E, D], F32, name="out_sb")
         nc.vector.tensor_scalar_mul(out_sb[:], mixed[:], recip[:])
         nc.sync.dma_start(out, out_sb[:])

@@ -45,21 +45,22 @@ def tile_radixattention_kernel(tc, q, pool_k, k, vals, offs, out):
         neg_scaled = held.tile([E, N + E], F32, name="neg_scaled")
         shift = held.tile([E, 1], F32, name="shift")
         nc.vector.tensor_scalar(neg_scaled[:], scores[:], -SCALE, None, op0=ALU.mult, op1=ALU.min, accum_out=shift[:])
-        weights = held.tile([E, N + E], BF16, name="weights")
-        denom = held.tile([E, 1], F32, name="denom")
-        nc.scalar.activation(weights[:], neg_scaled[:], EXP, bias=shift[:], scale=-1.0, accum_out=denom[:])
-        recip = held.tile([E, 1], F32, name="recip")
-        nc.vector.reciprocal(recip[:], denom[:])
-
-        weights_t_ps = psum.tile([128, 2, E], BF16, name="weights_t_ps")
-        for h in range(2):
-            nc.tensor.transpose(weights_t_ps[:, h, :], weights[:, h * 128 : (h + 1) * 128], ident[:])
-        weights_t = held.tile([128, 2, E], BF16, name="weights_t")
-        nc.vector.tensor_copy(weights_t[:], weights_t_ps[:])
+        weights = [held.tile([E, 128], BF16, name=f"weights{h}") for h in range(2)]
+        denom = [held.tile([E, 1], F32, name=f"denom{h}") for h in range(2)]
+        weights_t_ps = [psum.tile([128, E], BF16, name=f"weights_t_ps{h}") for h in range(2)]
+        weights_t = [held.tile([128, E], BF16, name=f"weights_t{h}") for h in range(2)]
         mixed = psum.tile([E, D], F32, name="mixed")
         for h in range(2):
-            nc.tensor.matmul(mixed[:], weights_t[:, h, :], vals_sb[:, h, :], start=(h == 0), stop=(h == 1))
+            nc.scalar.activation(
+                weights[h][:], neg_scaled[:, h * 128 : (h + 1) * 128], EXP, bias=shift[:], scale=-1.0, accum_out=denom[h][:]
+            )
+            nc.tensor.transpose(weights_t_ps[h][:], weights[h][:], ident[:])
+            nc.vector.tensor_copy(weights_t[h][:], weights_t_ps[h][:])
+            nc.tensor.matmul(mixed[:], weights_t[h][:], vals_sb[:, h, :], start=(h == 0), stop=(h == 1))
 
+        recip = held.tile([E, 1], F32, name="recip")
+        nc.vector.tensor_add(recip[:], denom[0][:], denom[1][:])
+        nc.vector.reciprocal(recip[:], recip[:])
         out_sb = held.tile([E, D], F32, name="out_sb")
         nc.vector.tensor_scalar_mul(out_sb[:], mixed[:], recip[:])
         nc.sync.dma_start(out, out_sb[:])

@@ -1,7 +1,6 @@
 import math
 
 import concourse.mybir as mybir
-from concourse.masks import make_identity
 
 D, S, N, E = 128, 256, 128, 128
 SCALE = 1.0 / math.sqrt(D)
@@ -11,7 +10,9 @@ FLOPS = 2 * E * (N + E) * D + 2 * E * (N + E) * D
 BF16, F32, I32, U16 = mybir.dt.bfloat16, mybir.dt.float32, mybir.dt.int32, mybir.dt.uint16
 ALU = mybir.AluOpType
 EXP = mybir.ActivationFunctionType.Exp
-X = mybir.AxisListType.X
+
+PART_COLUMNS = (slice(0, N), slice(N, N + E))
+
 
 def tile_radixattention_kernel(tc, q, pool_k, k, vals, offs, out):
     nc = tc.nc
@@ -30,37 +31,43 @@ def tile_radixattention_kernel(tc, q, pool_k, k, vals, offs, out):
         vals_sb = held.tile([128, 2, D], BF16, name="vals_sb")
         nc.sync.dma_start(vals_sb[:], vals.rearrange("(h j) d -> j h d", h=2))
 
-        ident = held.tile([128, 128], BF16, name="ident")
-        make_identity(nc, ident[:])
         ahead = held.tile([E, E], I32, name="ahead")
         nc.gpsimd.iota(ahead[:], pattern=[[-1, E]], base=0, channel_multiplier=1)
         causal = held.tile([E, E], BF16, name="causal")
         nc.vector.tensor_scalar(causal[:], ahead[:], 0.0, MASKED, op0=ALU.is_lt, op1=ALU.mult)
+        ident = held.tile([E, E], BF16, name="ident")
+        nc.vector.tensor_scalar(ident[:], ahead[:], 0.0, None, op0=ALU.is_equal)
 
         scores = psum.tile([E, N + E], F32, name="scores")
-        nc.tensor.matmul(scores[:, N:], ident[:], causal[:], start=True, stop=False)
-        nc.tensor.matmul(scores[:, N:], q_sb[:], k_sb[:], start=False, stop=True)
-        nc.tensor.matmul(scores[:, :N], q_sb[:], pool_sb[:].indirect(offsets[:]), start=True, stop=True)
+        nc.tensor.matmul(scores[:, PART_COLUMNS[1]], ident[:], causal[:], start=True, stop=False)
+        nc.tensor.matmul(scores[:, PART_COLUMNS[1]], q_sb[:], k_sb[:], start=False, stop=True)
+        nc.tensor.matmul(
+            scores[:, PART_COLUMNS[0]], q_sb[:], pool_sb[:].indirect(offsets[:]), start=True, stop=True
+        )
 
         neg_scaled = held.tile([E, N + E], F32, name="neg_scaled")
         shift = held.tile([E, 1], F32, name="shift")
-        nc.vector.tensor_scalar(neg_scaled[:], scores[:], -SCALE, None, op0=ALU.mult, op1=ALU.min, accum_out=shift[:])
-        weights = [held.tile([E, 128], BF16, name=f"weights{h}") for h in range(2)]
+        nc.vector.tensor_scalar(
+            neg_scaled[:], scores[:], -SCALE, None, op0=ALU.mult, op1=ALU.min, accum_out=shift[:]
+        )
+
+        weights = [held.tile([E, E], BF16, name=f"weights{h}") for h in range(2)]
         denom = [held.tile([E, 1], F32, name=f"denom{h}") for h in range(2)]
-        weights_t_ps = [psum.tile([128, E], BF16, name=f"weights_t_ps{h}") for h in range(2)]
-        weights_t = [held.tile([128, E], BF16, name=f"weights_t{h}") for h in range(2)]
+        weights_t_ps = [psum.tile([E, E], BF16, name=f"weights_t_ps{h}") for h in range(2)]
+        weights_t = [held.tile([E, E], BF16, name=f"weights_t{h}") for h in range(2)]
         mixed = psum.tile([E, D], F32, name="mixed")
         for h in range(2):
             nc.scalar.activation(
-                weights[h][:], neg_scaled[:, h * 128 : (h + 1) * 128], EXP, bias=shift[:], scale=-1.0, accum_out=denom[h][:]
+                weights[h][:], neg_scaled[:, PART_COLUMNS[h]], EXP, bias=shift[:], scale=-1.0, accum_out=denom[h][:]
             )
             nc.tensor.transpose(weights_t_ps[h][:], weights[h][:], ident[:])
             nc.vector.tensor_copy(weights_t[h][:], weights_t_ps[h][:])
             nc.tensor.matmul(mixed[:], weights_t[h][:], vals_sb[:, h, :], start=(h == 0), stop=(h == 1))
 
+        denom_sum = held.tile([E, 1], F32, name="denom_sum")
+        nc.vector.tensor_add(denom_sum[:], denom[0][:], denom[1][:])
         recip = held.tile([E, 1], F32, name="recip")
-        nc.vector.tensor_add(recip[:], denom[0][:], denom[1][:])
-        nc.vector.reciprocal(recip[:], recip[:])
+        nc.vector.reciprocal(recip[:], denom_sum[:])
         out_sb = held.tile([E, D], F32, name="out_sb")
         nc.vector.tensor_scalar_mul(out_sb[:], mixed[:], recip[:])
         nc.sync.dma_start(out, out_sb[:])

@@ -52,22 +52,21 @@ def tile_radixattention_kernel(tc, q, pool_k, k, vals, offs, out):
         )
 
         weights = [held.tile([E, E], BF16, name=f"weights{h}") for h in range(2)]
-        denom = [held.tile([E, 1], F32, name=f"denom{h}") for h in range(2)]
         weights_t_ps = [psum.tile([E, E], BF16, name=f"weights_t_ps{h}") for h in range(2)]
         weights_t = [held.tile([E, E], BF16, name=f"weights_t{h}") for h in range(2)]
         mixed = psum.tile([E, D], F32, name="mixed")
         for h in range(2):
-            nc.scalar.activation(
-                weights[h][:], neg_scaled[:, PART_COLUMNS[h]], EXP, bias=shift[:], scale=-1.0, accum_out=denom[h][:]
-            )
+            nc.scalar.activation(weights[h][:], neg_scaled[:, PART_COLUMNS[h]], EXP, bias=shift[:], scale=-1.0)
             nc.tensor.transpose(weights_t_ps[h][:], weights[h][:], ident[:])
             nc.vector.tensor_copy(weights_t[h][:], weights_t_ps[h][:])
             nc.tensor.matmul(mixed[:], weights_t[h][:], vals_sb[:, h, :], start=(h == 0), stop=(h == 1))
 
-        denom_sum = held.tile([E, 1], F32, name="denom_sum")
-        nc.vector.tensor_add(denom_sum[:], denom[0][:], denom[1][:])
+        exps = held.tile([E, N + E], F32, name="exps")
+        denom = held.tile([E, 1], F32, name="denom")
+        nc.scalar.activation(exps[:], neg_scaled[:], EXP, bias=shift[:], scale=-1.0, accum_out=denom[:])
         recip = held.tile([E, 1], F32, name="recip")
-        nc.vector.reciprocal(recip[:], denom_sum[:])
+        nc.vector.reciprocal(recip[:], denom[:])
+
         out_sb = held.tile([E, D], F32, name="out_sb")
         nc.vector.tensor_scalar_mul(out_sb[:], mixed[:], recip[:])
         nc.sync.dma_start(out, out_sb[:])

@@ -57,7 +57,7 @@ def tile_radixattention_kernel(tc, q, pool_k, k, vals, offs, out):
         mixed = psum.tile([E, D], F32, name="mixed")
         for h in range(2):
             nc.scalar.activation(weights[h][:], neg_scaled[:, PART_COLUMNS[h]], EXP, bias=shift[:], scale=-1.0)
-            nc.tensor.transpose(weights_t_ps[h][:], weights[h][:], ident[:])
+            nc.tensor.matmul(weights_t_ps[h][:], weights[h][:], ident[:], start=True, stop=True)
             nc.vector.tensor_copy(weights_t[h][:], weights_t_ps[h][:])
             nc.tensor.matmul(mixed[:], weights_t[h][:], vals_sb[:, h, :], start=(h == 0), stop=(h == 1))
 

@@ -7,7 +7,9 @@ SCALE = 1.0 / math.sqrt(D)
 MASKED = -1.0e30
 FLOPS = 2 * E * (N + E) * D + 2 * E * (N + E) * D
 
-BF16, F32, I32, U16 = mybir.dt.bfloat16, mybir.dt.float32, mybir.dt.int32, mybir.dt.uint16
+QUERY_COLUMNS = 16
+
+BF16, F32, U16 = mybir.dt.bfloat16, mybir.dt.float32, mybir.dt.uint16
 ALU = mybir.AluOpType
 EXP = mybir.ActivationFunctionType.Exp
 
@@ -31,24 +33,33 @@ def tile_radixattention_kernel(tc, q, pool_k, k, vals, offs, out):
         vals_sb = held.tile([128, 2, D], BF16, name="vals_sb")
         nc.sync.dma_start(vals_sb[:], vals.rearrange("(h j) d -> j h d", h=2))
 
-        ahead = held.tile([E, E], I32, name="ahead")
-        nc.gpsimd.iota(ahead[:], pattern=[[-1, E]], base=0, channel_multiplier=1)
+        ones = held.tile([E, E], F32, name="ones")
+        nc.vector.memset(ones[:], 1.0)
+        token = held.tile([E, E], BF16, name="token")
+        nc.vector.tensor_tensor_scan(token[:], ones[:], ones[:], -1.0, ALU.mult, ALU.add)
+        share = held.tile([E, QUERY_COLUMNS], BF16, name="share")
+        nc.gpsimd.memset(share[:], 1.0 / E)
+        query = psum.tile([E, QUERY_COLUMNS], F32, name="query")
+        nc.tensor.matmul(query[:], token[:], share[:], start=True, stop=True)
         causal = held.tile([E, E], BF16, name="causal")
-        nc.vector.tensor_scalar(causal[:], ahead[:], 0.0, MASKED, op0=ALU.is_lt, op1=ALU.mult)
+        nc.vector.tensor_scalar(causal[:], token[:], query[:, 0:1], MASKED, op0=ALU.is_gt, op1=ALU.mult)
         ident = held.tile([E, E], BF16, name="ident")
-        nc.vector.tensor_scalar(ident[:], ahead[:], 0.0, None, op0=ALU.is_equal)
+        nc.vector.tensor_scalar(ident[:], token[:], query[:, 0:1], None, op0=ALU.is_equal)
 
-        scores = psum.tile([E, N + E], F32, name="scores")
-        nc.tensor.matmul(scores[:, PART_COLUMNS[1]], ident[:], causal[:], start=True, stop=False)
-        nc.tensor.matmul(scores[:, PART_COLUMNS[1]], q_sb[:], k_sb[:], start=False, stop=True)
-        nc.tensor.matmul(
-            scores[:, PART_COLUMNS[0]], q_sb[:], pool_sb[:].indirect(offsets[:]), start=True, stop=True
-        )
+        scores_new = psum.tile([E, E], F32, name="scores_new")
+        scores_old = psum.tile([E, N], F32, name="scores_old")
+        nc.tensor.matmul(scores_new[:], ident[:], causal[:], start=True, stop=False)
+        nc.tensor.matmul(scores_new[:], q_sb[:], k_sb[:], start=False, stop=True)
+        nc.tensor.matmul(scores_old[:], q_sb[:], pool_sb[:].indirect(offsets[:]), start=True, stop=True)
 
         neg_scaled = held.tile([E, N + E], F32, name="neg_scaled")
+        shift_new = held.tile([E, 1], F32, name="shift_new")
+        nc.vector.tensor_scalar(
+            neg_scaled[:, PART_COLUMNS[1]], scores_new[:], -SCALE, None, op0=ALU.mult, op1=ALU.min, accum_out=shift_new[:]
+        )
         shift = held.tile([E, 1], F32, name="shift")
         nc.vector.tensor_scalar(
-            neg_scaled[:], scores[:], -SCALE, None, op0=ALU.mult, op1=ALU.min, accum_out=shift[:]
+            neg_scaled[:, PART_COLUMNS[0]], scores_old[:], -SCALE, shift_new[:], op0=ALU.mult, op1=ALU.min, accum_out=shift[:]
         )
 
         weights = [held.tile([E, E], BF16, name=f"weights{h}") for h in range(2)]

@@ -33,10 +33,11 @@ def tile_radixattention_kernel(tc, q, pool_k, k, vals, offs, out):
         vals_sb = held.tile([128, 2, D], BF16, name="vals_sb")
         nc.sync.dma_start(vals_sb[:], vals.rearrange("(h j) d -> j h d", h=2))
 
-        ones = held.tile([E, E], F32, name="ones")
-        nc.vector.memset(ones[:], 1.0)
+        one = held.tile([E, 1], F32, name="one")
+        nc.vector.memset(one[:], 1.0)
+        ones = one[:].to_broadcast([E, E])
         token = held.tile([E, E], BF16, name="token")
-        nc.vector.tensor_tensor_scan(token[:], ones[:], ones[:], -1.0, ALU.mult, ALU.add)
+        nc.vector.tensor_tensor_scan(token[:], ones, ones, -1.0, ALU.mult, ALU.add)
         share = held.tile([E, QUERY_COLUMNS], BF16, name="share")
         nc.gpsimd.memset(share[:], 1.0 / E)
         query = psum.tile([E, QUERY_COLUMNS], F32, name="query")

@@ -14,6 +14,7 @@ ALU = mybir.AluOpType
 EXP = mybir.ActivationFunctionType.Exp
 
 PART_COLUMNS = (slice(0, N), slice(N, N + E))
+HALF_FEATURES = (slice(0, D // 2), slice(D // 2, D))
 
 
 def tile_radixattention_kernel(tc, q, pool_k, k, vals, offs, out):
@@ -66,12 +67,15 @@ def tile_radixattention_kernel(tc, q, pool_k, k, vals, offs, out):
         weights = [held.tile([E, E], BF16, name=f"weights{h}") for h in range(2)]
         weights_t_ps = [psum.tile([E, E], BF16, name=f"weights_t_ps{h}") for h in range(2)]
         weights_t = [held.tile([E, E], BF16, name=f"weights_t{h}") for h in range(2)]
-        mixed = psum.tile([E, D], F32, name="mixed")
+        mixed = [psum.tile([E, D // 2], F32, name=f"mixed{c}") for c in range(2)]
         for h in range(2):
             nc.scalar.activation(weights[h][:], neg_scaled[:, PART_COLUMNS[h]], EXP, bias=shift[:], scale=-1.0)
             nc.tensor.matmul(weights_t_ps[h][:], weights[h][:], ident[:], start=True, stop=True)
             nc.vector.tensor_copy(weights_t[h][:], weights_t_ps[h][:])
-            nc.tensor.matmul(mixed[:], weights_t[h][:], vals_sb[:, h, :], start=(h == 0), stop=(h == 1))
+            for c in range(2):
+                nc.tensor.matmul(
+                    mixed[c][:], weights_t[h][:], vals_sb[:, h, HALF_FEATURES[c]], start=(h == 0), stop=(h == 1)
+                )
 
         exps = held.tile([E, N + E], F32, name="exps")
         denom = held.tile([E, 1], F32, name="denom")
@@ -80,5 +84,6 @@ def tile_radixattention_kernel(tc, q, pool_k, k, vals, offs, out):
         nc.vector.reciprocal(recip[:], denom[:])
 
         out_sb = held.tile([E, D], F32, name="out_sb")
-        nc.vector.tensor_scalar_mul(out_sb[:], mixed[:], recip[:])
+        for c in range(2):
+            nc.vector.tensor_scalar_mul(out_sb[:, HALF_FEATURES[c]], mixed[c][:], recip[:])
         nc.sync.dma_start(out, out_sb[:])

import math

import concourse.mybir as mybir

D, S, N, E = 128, 256, 128, 128
SCALE = 1.0 / math.sqrt(D)
MASKED = -1.0e30
FLOPS = 2 * E * (N + E) * D + 2 * E * (N + E) * D

QUERY_COLUMNS = 16

BF16, F32, U16 = mybir.dt.bfloat16, mybir.dt.float32, mybir.dt.uint16
ALU = mybir.AluOpType
EXP = mybir.ActivationFunctionType.Exp

PART_COLUMNS = (slice(0, N), slice(N, N + E))
HALF_FEATURES = (slice(0, D // 2), slice(D // 2, D))


def tile_radixattention_kernel(tc, q, pool_k, k, vals, offs, out):
    nc = tc.nc
    with (
        tc.tile_pool(name="held", bufs=1) as held,
        tc.psum_pool(name="psum", bufs=1) as psum,
    ):
        q_sb = held.tile([D, E], BF16, name="q_sb")
        nc.sync.dma_start(q_sb[:], q)
        k_sb = held.tile([D, E], BF16, name="k_sb")
        nc.scalar.dma_start(k_sb[:], k)
        offsets = held.tile([128, N // 16], U16, name="offsets")
        nc.sync.dma_start(offsets[:], offs)
        pool_sb = held.tile([D, S], BF16, name="pool_sb")
        nc.scalar.dma_start(pool_sb[:], pool_k)
        vals_sb = held.tile([128, 2, D], BF16, name="vals_sb")
        nc.sync.dma_start(vals_sb[:], vals.rearrange("(h j) d -> j h d", h=2))

        one = held.tile([E, 1], F32, name="one")
        nc.vector.memset(one[:], 1.0)
        ones = one[:].to_broadcast([E, E])
        token = held.tile([E, E], BF16, name="token")
        nc.vector.tensor_tensor_scan(token[:], ones, ones, -1.0, ALU.mult, ALU.add)
        share = held.tile([E, QUERY_COLUMNS], BF16, name="share")
        nc.gpsimd.memset(share[:], 1.0 / E)
        query = psum.tile([E, QUERY_COLUMNS], F32, name="query")
        nc.tensor.matmul(query[:], token[:], share[:], start=True, stop=True)
        causal = held.tile([E, E], BF16, name="causal")
        nc.vector.tensor_scalar(causal[:], token[:], query[:, 0:1], MASKED, op0=ALU.is_gt, op1=ALU.mult)
        ident = held.tile([E, E], BF16, name="ident")
        nc.vector.tensor_scalar(ident[:], token[:], query[:, 0:1], None, op0=ALU.is_equal)

        scores_new = psum.tile([E, E], F32, name="scores_new")
        scores_old = psum.tile([E, N], F32, name="scores_old")
        nc.tensor.matmul(scores_new[:], ident[:], causal[:], start=True, stop=False)
        nc.tensor.matmul(scores_new[:], q_sb[:], k_sb[:], start=False, stop=True)
        nc.tensor.matmul(scores_old[:], q_sb[:], pool_sb[:].indirect(offsets[:]), start=True, stop=True)

        neg_scaled = held.tile([E, N + E], F32, name="neg_scaled")
        shift_new = held.tile([E, 1], F32, name="shift_new")
        nc.vector.tensor_scalar(
            neg_scaled[:, PART_COLUMNS[1]], scores_new[:], -SCALE, None, op0=ALU.mult, op1=ALU.min, accum_out=shift_new[:]
        )
        shift = held.tile([E, 1], F32, name="shift")
        nc.vector.tensor_scalar(
            neg_scaled[:, PART_COLUMNS[0]], scores_old[:], -SCALE, shift_new[:], op0=ALU.mult, op1=ALU.min, accum_out=shift[:]
        )

        weights = [held.tile([E, E], BF16, name=f"weights{h}") for h in range(2)]
        weights_t_ps = [psum.tile([E, E], BF16, name=f"weights_t_ps{h}") for h in range(2)]
        weights_t = [held.tile([E, E], BF16, name=f"weights_t{h}") for h in range(2)]
        mixed = [psum.tile([E, D // 2], F32, name=f"mixed{c}") for c in range(2)]
        for h in range(2):
            nc.scalar.activation(weights[h][:], neg_scaled[:, PART_COLUMNS[h]], EXP, bias=shift[:], scale=-1.0)
            nc.tensor.matmul(weights_t_ps[h][:], weights[h][:], ident[:], start=True, stop=True)
            nc.vector.tensor_copy(weights_t[h][:], weights_t_ps[h][:])
            for c in range(2):
                nc.tensor.matmul(
                    mixed[c][:], weights_t[h][:], vals_sb[:, h, HALF_FEATURES[c]], start=(h == 0), stop=(h == 1)
                )

        exps = held.tile([E, N + E], F32, name="exps")
        denom = held.tile([E, 1], F32, name="denom")
        nc.scalar.activation(exps[:], neg_scaled[:], EXP, bias=shift[:], scale=-1.0, accum_out=denom[:])
        recip = held.tile([E, 1], F32, name="recip")
        nc.vector.reciprocal(recip[:], denom[:])

        out_sb = held.tile([E, D], F32, name="out_sb")
        for c in range(2):
            nc.vector.tensor_scalar_mul(out_sb[:, HALF_FEATURES[c]], mixed[c][:], recip[:])
        nc.sync.dma_start(out, out_sb[:])
